import numpy as np
import ml_dtypes


def mxq(x, axis, fmt="e4m3"):
    dtype, down = {"e4m3": (ml_dtypes.float8_e4m3fn, 7), "e5m2": (ml_dtypes.float8_e5m2, 14)}[fmt]
    v = np.moveaxis(np.asarray(x, np.float32).astype(ml_dtypes.bfloat16).astype(np.float64), axis, -1)
    blocks = v.reshape(v.shape[:-1] + (-1, 32))
    amax = np.abs(blocks).max(-1, keepdims=True)
    byte = np.maximum(np.where(amax > 0, np.frexp(amax)[1] - 1 + 127, 0) - down, 1)
    scale = np.exp2(byte - 127.0)
    codes = (blocks / scale).astype(np.float32).astype(dtype).astype(np.float64)
    return np.moveaxis((codes * scale).reshape(v.shape), -1, axis)


WIDE = False


def mx_kscale(k):
    if not WIDE:
        return np.ones(k)
    levels = np.array([10, -10, 5, -5, 0])
    if k % 512:
        return np.exp2(np.random.permutation(np.resize(levels, k // 32))).repeat(32)
    a = np.empty((k // 512, 16))
    for p in range(k // 512):
        a[p, :8] = np.random.permutation(np.resize(levels, 8))
        for g in range(8):
            far = levels[np.abs(levels - a[p, g]) >= 10]
            a[p, g + 8] = far[np.random.randint(len(far))]
    return np.exp2(a.ravel()).repeat(32)


BF16 = ml_dtypes.bfloat16


def bf(x):
    return np.asarray(x, np.float32).astype(BF16)


def f64(x):
    return np.asarray(x).astype(np.float64)


B, A, E, P, R = 256, 8, 512, 512, 512


def draw0():
    s = mx_kscale(R)
    return {
        "attr_rep": bf(np.random.standard_normal((B, A, R)) * s),
        "bwd_proj": bf(np.random.standard_normal((A, R, P)) / np.sqrt(R) / s[:, None]),
        "self_weighted": bf(1.0 + 0.3 * np.random.standard_normal((1, A, 1))),
    }


def core(attr_rep, bwd_proj, self_weighted):
    proj = (mxq(f64(attr_rep).transpose(1, 0, 2), 2, "e4m3") @ mxq(f64(bwd_proj), 1, "e4m3")).transpose(1, 0, 2)
    return np.sum(np.maximum(proj, 0.0) * f64(self_weighted), axis=1)


def e4m3fn_bytes(y):
    return np.clip(np.asarray(y, np.float64), -448.0, 448.0).astype(np.float32).astype(ml_dtypes.float8_e4m3fn).view(np.uint8)


def e4m3fn_values(b):
    return np.asarray(b, np.uint8).view(ml_dtypes.float8_e4m3fn).astype(np.float64)


def setup_inputs():
    d = draw0()
    x0 = np.asarray(d['bwd_proj']).astype(np.float64)
    s = (np.max(np.abs(x0), axis=(0, 2), keepdims=True) / 448.0).astype(np.float32)
    out = {}
    for k, v in d.items():
        if k == 'bwd_proj':
            out['bwd_proj_bytes'] = e4m3fn_bytes(x0 / s.astype(np.float64))
            out['bwd_proj_scale'] = s
        else:
            out[k] = v
    return out


def reference(attr_rep, bwd_proj_bytes, bwd_proj_scale, self_weighted):
    return core(attr_rep, e4m3fn_values(bwd_proj_bytes) * bwd_proj_scale.astype(np.float64), self_weighted)

@@ -1,0 +1,190 @@
+from contextlib import ExitStack
+
+import concourse.mybir as mybir
+from concourse.masks import make_identity
+
+B, A, R, P = 256, 8, 512, 512
+FLOPS = 2 * B * A * R * P
+
+F32 = mybir.dt.float32
+BF16 = mybir.dt.bfloat16
+U32 = mybir.dt.uint32
+U8 = mybir.dt.uint8
+FP8 = mybir.dt.float8_e4m3fn
+FP8X4 = mybir.dt.float8_e4m3fn_x4
+ALU = mybir.AluOpType
+ACT = mybir.ActivationFunctionType
+
+NP = 128
+PACK = 4
+BT = B // NP
+
+S_PLANES = (1, 3, 3, 3, 3, 3, 3, 4)
+
+
+def tile_attributegnn_pb_kernel(tc, attr_rep, bwd_proj_bytes, bwd_proj_scale, self_weighted, out):
+    nc = tc.nc
+    with ExitStack() as ctx:
+        const = ctx.enter_context(tc.tile_pool(name="const", bufs=1))
+        resident = ctx.enter_context(tc.tile_pool(name="resident", bufs=1))
+        rot2 = ctx.enter_context(tc.tile_pool(name="rot2", bufs=2))
+        rot4 = ctx.enter_context(tc.tile_pool(name="rot4", bufs=4))
+        psum_x = ctx.enter_context(tc.psum_pool(name="psum_x", bufs=2))
+        psum_p = ctx.enter_context(tc.psum_pool(name="psum_p", bufs=4))
+        ctx.enter_context(tc.manual_schedule())
+
+        k_scale = const.tile([NP, PACK], F32, name="k_scale")
+        nc.sync.dma_start(out=k_scale[:], in_=bwd_proj_scale.rearrange("o (p t) u -> p (o t u)", t=PACK))
+        w_bf = const.tile([NP, A], BF16, name="w_bf")
+        x_view = attr_rep.rearrange("(bt p) a k -> p bt a k", p=NP)
+        w_bytes = []
+        x_rows = []
+        for a in range(A):
+            wb = resident.tile([NP, PACK * P], U8, name="w_bytes%d" % a)
+            nc.sync.dma_start(out=wb[:], in_=bwd_proj_bytes[a].rearrange("(p t) n -> p (t n)", t=PACK))
+            w_bytes.append(wb)
+            xr = resident.tile([NP, BT, R], BF16, name="x_rows%d" % a)
+            nc.sync.dma_start(out=xr[:], in_=x_view[:, :, a, :])
+            x_rows.append(xr)
+            if a == 0:
+                nc.sync.dma_start(
+                    out=w_bf[:], in_=self_weighted.rearrange("o a u -> (o a u)").partition_broadcast(NP)
+                )
+
+        ident = const.tile([NP, NP], F32, name="ident")
+        make_identity(nc, ident[:])
+        warm_in = const.tile([NP, 1], F32, name="warm_in")
+        warm_out = const.tile([NP, 1], F32, name="warm_out")
+        nc.vector.memset(warm_in[:], 0.0)
+        nc.scalar.activation(out=warm_out[:], in_=warm_in[:], func=ACT.Relu)
+        w_f32 = const.tile([NP, A], F32, name="w_f32")
+        acc = [const.tile([NP, P], F32, name="acc%d" % bt) for bt in range(BT)]
+
+        planes = {}
+        w_group = {}
+        w_codes = {}
+        w_scales = {}
+        x_t = {}
+        x_group = {}
+        x_codes = {}
+        x_scales = {}
+        prod = {}
+        relu = {}
+
+        def widen_alloc(a):
+            planes[a] = rot2.tile([NP, PACK, P], BF16, name="planes", tag="planes")
+
+        def widen_scalar(a):
+            for t in range(S_PLANES[a]):
+                nc.scalar.activation(
+                    out=planes[a][:, t, :],
+                    in_=w_bytes[a][:, t * P : (t + 1) * P].bitcast(FP8),
+                    func=ACT.Copy,
+                    scale=k_scale[:, t : t + 1],
+                )
+
+        def widen_vector(a):
+            for t in range(S_PLANES[a], PACK):
+                nc.vector.tensor_scalar(
+                    out=planes[a][:, t, :],
+                    in0=w_bytes[a][:, t * P : (t + 1) * P].bitcast(FP8),
+                    scalar1=k_scale[:, t : t + 1],
+                    scalar2=None,
+                    op0=ALU.mult,
+                )
+
+        def interleave(a):
+            w_group[a] = rot2.tile([NP, P, PACK], BF16, name="w_group", tag="w_group", align_bytes=64)
+            nc.vector.tensor_copy(out=w_group[a][:], in_=planes[a][:].rearrange("p t n -> p n t"))
+
+        def quant_w(a):
+            w_codes[a] = rot2.tile([NP, P], U32, name="w_codes", tag="w_codes", align_bytes=64)
+            w_scales[a] = rot2.tile([NP, P], U8, name="w_scales", tag="w_scales", align_bytes=64)
+            nc.vector.quantize_mx(
+                out=w_codes[a][:].bitcast(FP8X4),
+                scales=w_scales[a][:],
+                in_=w_group[a][:].rearrange("p n t -> p (n t)"),
+            )
+
+        def transposes(a):
+            x_t[a] = psum_x.tile([NP, 2, B], F32, name="x_t", tag="x_t")
+            for bt in range(BT):
+                words = x_rows[a][:, bt, :].bitcast(F32)
+                for u in range(2):
+                    nc.tensor.transpose(x_t[a][:, u, bt * NP : (bt + 1) * NP], words[:, u : R // 2 : 2], ident[:])
+
+        def x_copy(a):
+            x_group[a] = rot2.tile([NP, B * PACK], BF16, name="x_group", tag="x_group", align_bytes=64)
+            nc.scalar.copy(
+                out=x_group[a][:].bitcast(F32).rearrange("p (b u) -> p b u", u=2),
+                in_=x_t[a][:].rearrange("p u b -> p b u"),
+            )
+
+        def quant_x(a):
+            x_codes[a] = rot2.tile([NP, B], U32, name="x_codes", tag="x_codes", align_bytes=64)
+            x_scales[a] = rot2.tile([NP, B], U8, name="x_scales", tag="x_scales", align_bytes=64)
+            nc.vector.quantize_mx(out=x_codes[a][:].bitcast(FP8X4), scales=x_scales[a][:], in_=x_group[a][:])
+
+        def matmuls(a):
+            for bt in range(BT):
+                cols = slice(bt * NP, (bt + 1) * NP)
+                prod[a, bt] = psum_p.tile([NP, P], F32, name="prod", tag="prod")
+                nc.tensor.matmul_mx(
+                    out=prod[a, bt][:],
+                    lhsT=x_codes[a][:, cols].bitcast(FP8X4),
+                    lhsT_scale=x_scales[a][:, cols],
+                    rhs=w_codes[a][:].bitcast(FP8X4),
+                    rhs_scale=w_scales[a][:],
+                    start=True,
+                    stop=True,
+                )
+
+        def relus(a):
+            if a == 0:
+                return
+            for bt in range(BT):
+                relu[a, bt] = rot4.tile([NP, P], F32, name="relu", tag="relu")
+                nc.scalar.activation(out=relu[a, bt][:], in_=prod[a, bt][:], func=ACT.Relu)
+
+        def accumulate(a):
+            for bt in range(BT):
+                if a == 0:
+                    nc.vector.tensor_scalar(
+                        out=acc[bt][:],
+                        in0=prod[a, bt][:],
+                        scalar1=0.0,
+                        scalar2=w_f32[:, 0:1],
+                        op0=ALU.max,
+                        op1=ALU.mult,
+                    )
+                else:
+                    nc.vector.scalar_tensor_tensor(
+                        out=acc[bt][:],
+                        in0=relu[a, bt][:],
+                        scalar=w_f32[:, a : a + 1],
+                        in1=acc[bt][:],
+                        op0=ALU.mult,
+                        op1=ALU.add,
+                    )
+                if a == A - 1:
+                    nc.sync.dma_start(out=out[bt * NP : (bt + 1) * NP, :], in_=acc[bt][:])
+
+        for i in range(-1, A + 1):
+            if 0 <= i < A:
+                interleave(i)
+                quant_x(i)
+            if 0 <= i - 1 < A:
+                relus(i - 1)
+            if i + 1 < A:
+                transposes(i + 1)
+                widen_alloc(i + 1)
+                widen_scalar(i + 1)
+                widen_vector(i + 1)
+                x_copy(i + 1)
+            if 0 <= i < A:
+                quant_w(i)
+                matmuls(i)
+            if i == 0:
+                nc.vector.tensor_copy(out=w_f32[:], in_=w_bf[:])
+            if 0 <= i - 1 < A:
+                accumulate(i - 1)

@@ -95,7 +95,10 @@ def tile_attributegnn_pb_kernel(tc, attr_rep, bwd_proj_bytes, bwd_proj_scale, se
 
         def interleave(a):
             w_group[a] = rot2.tile([NP, P, PACK], BF16, name="w_group", tag="w_group", align_bytes=64)
-            nc.vector.tensor_copy(out=w_group[a][:], in_=planes[a][:].rearrange("p t n -> p n t"))
+            nc.vector.tensor_copy(
+                out=w_group[a][:].rearrange("p (c i) t -> p c t i", i=4),
+                in_=planes[a][:].rearrange("p t (c i) -> p c t i", i=4),
+            )
 
         def quant_w(a):
             w_codes[a] = rot2.tile([NP, P], U32, name="w_codes", tag="w_codes", align_bytes=64)

@@ -18,8 +18,17 @@ ACT = mybir.ActivationFunctionType
 NP = 128
 PACK = 4
 BT = B // NP
+RUN = 4
 
-S_PLANES = (1, 3, 3, 3, 3, 3, 3, 4)
+PE_TYPES = 3
+S_PLANES = (1, 2, 2, 2, 2, 3, 3, 4)
+S_COLS = (0, 0, 0, 0, 0, 0, 0, 0)
+ACC_AT = {5: (3,), 6: (4,), 7: (5,), 8: (6,), 9: (7,)}
+X_AHEAD = 2
+DIAG_LAG = 2
+PRE = 1
+S_AHEAD = 2
+V_AHEAD = 1
 
 
 def tile_attributegnn_pb_kernel(tc, attr_rep, bwd_proj_bytes, bwd_proj_scale, self_weighted, out):
@@ -27,27 +36,31 @@ def tile_attributegnn_pb_kernel(tc, attr_rep, bwd_proj_bytes, bwd_proj_scale, se
     with ExitStack() as ctx:
         const = ctx.enter_context(tc.tile_pool(name="const", bufs=1))
         resident = ctx.enter_context(tc.tile_pool(name="resident", bufs=1))
-        rot2 = ctx.enter_context(tc.tile_pool(name="rot2", bufs=2))
-        rot4 = ctx.enter_context(tc.tile_pool(name="rot4", bufs=4))
         psum_x = ctx.enter_context(tc.psum_pool(name="psum_x", bufs=2))
         psum_p = ctx.enter_context(tc.psum_pool(name="psum_p", bufs=4))
+        psum_s = ctx.enter_context(tc.psum_pool(name="psum_s", bufs=1))
         ctx.enter_context(tc.manual_schedule())
 
         k_scale = const.tile([NP, PACK], F32, name="k_scale")
-        nc.sync.dma_start(out=k_scale[:], in_=bwd_proj_scale.rearrange("o (p t) u -> p (o t u)", t=PACK))
+        nc.scalar.dma_start(out=k_scale[:], in_=bwd_proj_scale.rearrange("o (p t) u -> p (o t u)", t=PACK))
         w_bf = const.tile([NP, A], BF16, name="w_bf")
         x_view = attr_rep.rearrange("(bt p) a k -> p bt a k", p=NP)
         w_bytes = []
         x_rows = []
         for a in range(A):
             wb = resident.tile([NP, PACK * P], U8, name="w_bytes%d" % a)
-            nc.sync.dma_start(out=wb[:], in_=bwd_proj_bytes[a].rearrange("(p t) n -> p (t n)", t=PACK))
+            src = bwd_proj_bytes[a].rearrange("(p t) n -> p (t n)", t=PACK)
+            if a == 0:
+                for t in range(PACK):
+                    nc.sync.dma_start(out=wb[:, t * P : (t + 1) * P], in_=src[:, t * P : (t + 1) * P])
+            else:
+                nc.sync.dma_start(out=wb[:], in_=src)
             w_bytes.append(wb)
             xr = resident.tile([NP, BT, R], BF16, name="x_rows%d" % a)
             nc.sync.dma_start(out=xr[:], in_=x_view[:, :, a, :])
             x_rows.append(xr)
             if a == 0:
-                nc.sync.dma_start(
+                nc.scalar.dma_start(
                     out=w_bf[:], in_=self_weighted.rearrange("o a u -> (o a u)").partition_broadcast(NP)
                 )
 
@@ -58,7 +71,16 @@ def tile_attributegnn_pb_kernel(tc, attr_rep, bwd_proj_bytes, bwd_proj_scale, se
         nc.vector.memset(warm_in[:], 0.0)
         nc.scalar.activation(out=warm_out[:], in_=warm_in[:], func=ACT.Relu)
         w_f32 = const.tile([NP, A], F32, name="w_f32")
-        acc = [const.tile([NP, P], F32, name="acc%d" % bt) for bt in range(BT)]
+        nc.gpsimd.tensor_copy(out=w_f32[:], in_=w_bf[:])
+        diag = []
+        for a in range(PE_TYPES):
+            dg = const.tile([NP, NP], F32, name="diag%d" % a)
+            nc.gpsimd.tensor_scalar(
+                out=dg[:], in0=ident[:], scalar1=w_f32[:, a : a + 1], scalar2=0.0, op0=ALU.mult, op1=ALU.add
+            )
+            diag.append(dg)
+        acc = const.tile([NP, BT, P], F32, name="acc")
+        pe_sum = [psum_s.tile([NP, P], F32, name="pe_sum%d" % bt) for bt in range(BT if PE_TYPES else 0)]
 
         planes = {}
         w_group = {}
@@ -71,38 +93,38 @@ def tile_attributegnn_pb_kernel(tc, attr_rep, bwd_proj_bytes, bwd_proj_scale, se
         prod = {}
         relu = {}
 
-        def widen_alloc(a):
-            planes[a] = rot2.tile([NP, PACK, P], BF16, name="planes", tag="planes")
+        def widen(a, lo, hi):
+            if a not in planes:
+                planes[a] = resident.tile([NP, PACK, P], BF16, name="planes%d" % a)
+            for t in range(lo, hi):
+                src = w_bytes[a][:, t * P : (t + 1) * P].bitcast(FP8)
+                if t < S_PLANES[a]:
+                    nc.scalar.activation(out=planes[a][:, t, :], in_=src, func=ACT.Copy, scale=k_scale[:, t : t + 1])
+                else:
+                    nc.vector.tensor_scalar(
+                        out=planes[a][:, t, :], in0=src, scalar1=k_scale[:, t : t + 1], scalar2=None, op0=ALU.mult
+                    )
 
-        def widen_scalar(a):
-            for t in range(S_PLANES[a]):
-                nc.scalar.activation(
-                    out=planes[a][:, t, :],
-                    in_=w_bytes[a][:, t * P : (t + 1) * P].bitcast(FP8),
-                    func=ACT.Copy,
-                    scale=k_scale[:, t : t + 1],
-                )
-
-        def widen_vector(a):
-            for t in range(S_PLANES[a], PACK):
-                nc.vector.tensor_scalar(
-                    out=planes[a][:, t, :],
-                    in0=w_bytes[a][:, t * P : (t + 1) * P].bitcast(FP8),
-                    scalar1=k_scale[:, t : t + 1],
-                    scalar2=None,
-                    op0=ALU.mult,
-                )
+        def in_range(a):
+            return 0 <= a < A
 
         def interleave(a):
-            w_group[a] = rot2.tile([NP, P, PACK], BF16, name="w_group", tag="w_group", align_bytes=64)
-            nc.vector.tensor_copy(
-                out=w_group[a][:].rearrange("p (c i) t -> p c t i", i=4),
-                in_=planes[a][:].rearrange("p t (c i) -> p c t i", i=4),
-            )
+            w_group[a] = resident.tile([NP, P, PACK], BF16, name="w_group%d" % a, align_bytes=64)
+            cut = S_COLS[a]
+            if cut < P:
+                nc.vector.tensor_copy(
+                    out=w_group[a][:, cut:P, :].rearrange("p (c i) t -> p c t i", i=RUN),
+                    in_=planes[a][:, :, cut:P].rearrange("p t (c i) -> p c t i", i=RUN),
+                )
+            if cut > 0:
+                nc.scalar.copy(
+                    out=w_group[a][:, 0:cut, :].rearrange("p (c i) t -> p c t i", i=RUN),
+                    in_=planes[a][:, :, 0:cut].rearrange("p t (c i) -> p c t i", i=RUN),
+                )
 
         def quant_w(a):
-            w_codes[a] = rot2.tile([NP, P], U32, name="w_codes", tag="w_codes", align_bytes=64)
-            w_scales[a] = rot2.tile([NP, P], U8, name="w_scales", tag="w_scales", align_bytes=64)
+            w_codes[a] = resident.tile([NP, P], U32, name="w_codes%d" % a, align_bytes=64)
+            w_scales[a] = resident.tile([NP, P], U8, name="w_scales%d" % a, align_bytes=64)
             nc.vector.quantize_mx(
                 out=w_codes[a][:].bitcast(FP8X4),
                 scales=w_scales[a][:],
@@ -117,15 +139,15 @@ def tile_attributegnn_pb_kernel(tc, attr_rep, bwd_proj_bytes, bwd_proj_scale, se
                     nc.tensor.transpose(x_t[a][:, u, bt * NP : (bt + 1) * NP], words[:, u : R // 2 : 2], ident[:])
 
         def x_copy(a):
-            x_group[a] = rot2.tile([NP, B * PACK], BF16, name="x_group", tag="x_group", align_bytes=64)
+            x_group[a] = resident.tile([NP, B * PACK], BF16, name="x_group%d" % a, align_bytes=64)
             nc.scalar.copy(
                 out=x_group[a][:].bitcast(F32).rearrange("p (b u) -> p b u", u=2),
                 in_=x_t[a][:].rearrange("p u b -> p b u"),
             )
 
         def quant_x(a):
-            x_codes[a] = rot2.tile([NP, B], U32, name="x_codes", tag="x_codes", align_bytes=64)
-            x_scales[a] = rot2.tile([NP, B], U8, name="x_scales", tag="x_scales", align_bytes=64)
+            x_codes[a] = resident.tile([NP, B], U32, name="x_codes%d" % a, align_bytes=64)
+            x_scales[a] = resident.tile([NP, B], U8, name="x_scales%d" % a, align_bytes=64)
             nc.vector.quantize_mx(out=x_codes[a][:].bitcast(FP8X4), scales=x_scales[a][:], in_=x_group[a][:])
 
         def matmuls(a):
@@ -143,51 +165,63 @@ def tile_attributegnn_pb_kernel(tc, attr_rep, bwd_proj_bytes, bwd_proj_scale, se
                 )
 
         def relus(a):
-            if a == 0:
+            if a == 0 and PE_TYPES == 0:
                 return
+            relu[a] = resident.tile([NP, BT, P], F32, name="relu%d" % a)
             for bt in range(BT):
-                relu[a, bt] = rot4.tile([NP, P], F32, name="relu", tag="relu")
-                nc.scalar.activation(out=relu[a, bt][:], in_=prod[a, bt][:], func=ACT.Relu)
+                nc.scalar.activation(out=relu[a][:, bt, :], in_=prod[a, bt][:], func=ACT.Relu)
+
+        def pe_add(a):
+            for bt in range(BT):
+                nc.tensor.matmul(
+                    out=pe_sum[bt][:], lhsT=diag[a][:], rhs=relu[a][:, bt, :], start=(a == 0), stop=(a == PE_TYPES - 1)
+                )
 
         def accumulate(a):
-            for bt in range(BT):
-                if a == 0:
+            w_col = w_f32[:, a : a + 1]
+            if a == 0:
+                for bt in range(BT):
                     nc.vector.tensor_scalar(
-                        out=acc[bt][:],
-                        in0=prod[a, bt][:],
-                        scalar1=0.0,
-                        scalar2=w_f32[:, 0:1],
-                        op0=ALU.max,
-                        op1=ALU.mult,
+                        out=acc[:, bt, :], in0=prod[a, bt][:], scalar1=0.0, scalar2=w_col, op0=ALU.max, op1=ALU.mult
                     )
-                else:
+            elif a == PE_TYPES or a == A - 1:
+                for bt in range(BT):
                     nc.vector.scalar_tensor_tensor(
-                        out=acc[bt][:],
-                        in0=relu[a, bt][:],
-                        scalar=w_f32[:, a : a + 1],
-                        in1=acc[bt][:],
+                        out=acc[:, bt, :],
+                        in0=relu[a][:, bt, :],
+                        scalar=w_col,
+                        in1=pe_sum[bt][:] if a == PE_TYPES else acc[:, bt, :],
                         op0=ALU.mult,
                         op1=ALU.add,
                     )
-                if a == A - 1:
-                    nc.sync.dma_start(out=out[bt * NP : (bt + 1) * NP, :], in_=acc[bt][:])
+                    if a == A - 1:
+                        nc.sync.dma_start(out=out[bt * NP : (bt + 1) * NP, :], in_=acc[:, bt, :])
+            else:
+                flat = acc[:].rearrange("p b n -> p (b n)")
+                nc.vector.scalar_tensor_tensor(
+                    out=flat, in0=relu[a][:].rearrange("p b n -> p (b n)"), scalar=w_col, in1=flat, op0=ALU.mult, op1=ALU.add
+                )
 
-        for i in range(-1, A + 1):
-            if 0 <= i < A:
+        for i in range(-max(X_AHEAD, S_AHEAD), A + 3):
+            if in_range(i):
                 interleave(i)
                 quant_x(i)
-            if 0 <= i - 1 < A:
+            if in_range(i + X_AHEAD):
+                transposes(i + X_AHEAD)
+            if in_range(i + S_AHEAD):
+                widen(i + S_AHEAD, 0, min(PRE, S_PLANES[i + S_AHEAD]))
+            if in_range(i - 1):
                 relus(i - 1)
-            if i + 1 < A:
-                transposes(i + 1)
-                widen_alloc(i + 1)
-                widen_scalar(i + 1)
-                widen_vector(i + 1)
-                x_copy(i + 1)
-            if 0 <= i < A:
+            if in_range(i + S_AHEAD):
+                widen(i + S_AHEAD, min(PRE, S_PLANES[i + S_AHEAD]), S_PLANES[i + S_AHEAD])
+            if in_range(i + V_AHEAD):
+                widen(i + V_AHEAD, S_PLANES[i + V_AHEAD], PACK)
+            if in_range(i + X_AHEAD):
+                x_copy(i + X_AHEAD)
+            if 0 <= i - DIAG_LAG < PE_TYPES:
+                pe_add(i - DIAG_LAG)
+            if in_range(i):
                 quant_w(i)
                 matmuls(i)
-            if i == 0:
-                nc.vector.tensor_copy(out=w_f32[:], in_=w_bf[:])
-            if 0 <= i - 1 < A:
-                accumulate(i - 1)
+            for a in ACC_AT.get(i, ()):
+                accumulate(a)

@@ -71,14 +71,13 @@ def tile_attributegnn_pb_kernel(tc, attr_rep, bwd_proj_bytes, bwd_proj_scale, se
         nc.vector.memset(warm_in[:], 0.0)
         nc.scalar.activation(out=warm_out[:], in_=warm_in[:], func=ACT.Relu)
         w_f32 = const.tile([NP, A], F32, name="w_f32")
-        nc.gpsimd.tensor_copy(out=w_f32[:], in_=w_bf[:])
-        diag = []
-        for a in range(PE_TYPES):
-            dg = const.tile([NP, NP], F32, name="diag%d" % a)
-            nc.gpsimd.tensor_scalar(
-                out=dg[:], in0=ident[:], scalar1=w_f32[:, a : a + 1], scalar2=0.0, op0=ALU.mult, op1=ALU.add
-            )
-            diag.append(dg)
+        diag = [const.tile([NP, NP], F32, name="diag%d" % a) for a in range(PE_TYPES)]
+
+        def weights():
+            nc.scalar.activation(out=w_f32[:], in_=w_bf[:], func=ACT.Copy)
+            for a in range(PE_TYPES):
+                nc.scalar.activation(out=diag[a][:], in_=ident[:], func=ACT.Copy, scale=w_f32[:, a : a + 1])
+
         acc = const.tile([NP, BT, P], F32, name="acc")
         pe_sum = [psum_s.tile([NP, P], F32, name="pe_sum%d" % bt) for bt in range(BT if PE_TYPES else 0)]
 
@@ -214,6 +213,8 @@ def tile_attributegnn_pb_kernel(tc, attr_rep, bwd_proj_bytes, bwd_proj_scale, se
                 relus(i - 1)
             if in_range(i + S_AHEAD):
                 widen(i + S_AHEAD, min(PRE, S_PLANES[i + S_AHEAD]), S_PLANES[i + S_AHEAD])
+            if i + S_AHEAD == 0:
+                weights()
             if in_range(i + V_AHEAD):
                 widen(i + V_AHEAD, S_PLANES[i + V_AHEAD], PACK)
             if in_range(i + X_AHEAD):

@@ -21,11 +21,12 @@ BT = B // NP
 RUN = 4
 
 PE_TYPES = 3
-S_PLANES = (1, 2, 2, 2, 2, 3, 3, 4)
+S_PLANES = (2, 1, 2, 2, 3, 3, 3, 4)
 S_COLS = (0, 0, 0, 0, 0, 0, 0, 0)
-ACC_AT = {5: (3,), 6: (4,), 7: (5,), 8: (6,), 9: (7,)}
+ACC_MID = {6: (3,)}
+ACC_END = {6: (4,), 7: (5,), 8: (6,), 9: (7,)}
 X_AHEAD = 2
-DIAG_LAG = 2
+PE_ADD_AT = {1: ((0, 0),), 2: ((0, 1), (1, 0)), 3: ((1, 1),), 4: ((2, 0), (2, 1))}
 PRE = 1
 S_AHEAD = 2
 V_AHEAD = 1
@@ -170,11 +171,10 @@ def tile_attributegnn_pb_kernel(tc, attr_rep, bwd_proj_bytes, bwd_proj_scale, se
             for bt in range(BT):
                 nc.scalar.activation(out=relu[a][:, bt, :], in_=prod[a, bt][:], func=ACT.Relu)
 
-        def pe_add(a):
-            for bt in range(BT):
-                nc.tensor.matmul(
-                    out=pe_sum[bt][:], lhsT=diag[a][:], rhs=relu[a][:, bt, :], start=(a == 0), stop=(a == PE_TYPES - 1)
-                )
+        def pe_add(a, bt):
+            nc.tensor.matmul(
+                out=pe_sum[bt][:], lhsT=diag[a][:], rhs=relu[a][:, bt, :], start=(a == 0), stop=(a == PE_TYPES - 1)
+            )
 
         def accumulate(a):
             w_col = w_f32[:, a : a + 1]
@@ -219,10 +219,12 @@ def tile_attributegnn_pb_kernel(tc, attr_rep, bwd_proj_bytes, bwd_proj_scale, se
                 widen(i + V_AHEAD, S_PLANES[i + V_AHEAD], PACK)
             if in_range(i + X_AHEAD):
                 x_copy(i + X_AHEAD)
-            if 0 <= i - DIAG_LAG < PE_TYPES:
-                pe_add(i - DIAG_LAG)
+            for a, bt in PE_ADD_AT.get(i, ()):
+                pe_add(a, bt)
+            for a in ACC_MID.get(i, ()):
+                accumulate(a)
             if in_range(i):
                 quant_w(i)
                 matmuls(i)
-            for a in ACC_AT.get(i, ()):
+            for a in ACC_END.get(i, ()):
                 accumulate(a)

@@ -18,18 +18,16 @@ ACT = mybir.ActivationFunctionType
 NP = 128
 PACK = 4
 BT = B // NP
+NT = P // NP
 RUN = 4
 
-PE_TYPES = 3
-S_PLANES = (2, 1, 2, 2, 3, 3, 3, 4)
-S_COLS = (0, 0, 0, 0, 0, 0, 0, 0)
-ACC_MID = {6: (3,)}
-ACC_END = {6: (4,), 7: (5,), 8: (6,), 9: (7,)}
+S_PLANES = (2, 2, 3, 3, 3, 3, 3, 3)
+ROAD = "DTDTDVVV"
+V_LAG = 2
 X_AHEAD = 2
-PE_ADD_AT = {1: ((0, 0),), 2: ((0, 1), (1, 0)), 3: ((1, 1),), 4: ((2, 0), (2, 1))}
-PRE = 1
 S_AHEAD = 2
 V_AHEAD = 1
+PRE = 1
 
 
 def tile_attributegnn_pb_kernel(tc, attr_rep, bwd_proj_bytes, bwd_proj_scale, self_weighted, out):
@@ -72,15 +70,18 @@ def tile_attributegnn_pb_kernel(tc, attr_rep, bwd_proj_bytes, bwd_proj_scale, se
         nc.vector.memset(warm_in[:], 0.0)
         nc.scalar.activation(out=warm_out[:], in_=warm_in[:], func=ACT.Relu)
         w_f32 = const.tile([NP, A], F32, name="w_f32")
-        diag = [const.tile([NP, NP], F32, name="diag%d" % a) for a in range(PE_TYPES)]
+        diag = dict((a, const.tile([NP, NP], F32, name="diag%d" % a)) for a in range(A) if ROAD[a] == "D")
 
         def weights():
             nc.scalar.activation(out=w_f32[:], in_=w_bf[:], func=ACT.Copy)
-            for a in range(PE_TYPES):
-                nc.scalar.activation(out=diag[a][:], in_=ident[:], func=ACT.Copy, scale=w_f32[:, a : a + 1])
 
-        acc = const.tile([NP, BT, P], F32, name="acc")
-        pe_sum = [psum_s.tile([NP, P], F32, name="pe_sum%d" % bt) for bt in range(BT if PE_TYPES else 0)]
+        def make_diag(a):
+            nc.scalar.activation(out=diag[a][:], in_=ident[:], func=ACT.Copy, scale=w_f32[:, a : a + 1])
+
+        out_sb = const.tile([NP, BT, P], F32, name="out_sb")
+        pe_sum = [psum_s.tile([NP, P], F32, name="pe_sum%d" % bt) for bt in range(BT)]
+        adds_total = [NT * ROAD.count("T") + ROAD.count("D")] * BT
+        adds_done = [0, 0]
 
         planes = {}
         w_group = {}
@@ -91,7 +92,10 @@ def tile_attributegnn_pb_kernel(tc, attr_rep, bwd_proj_bytes, bwd_proj_scale, se
         x_codes = {}
         x_scales = {}
         prod = {}
-        relu = {}
+        term = {}
+
+        def in_range(a):
+            return 0 <= a < A
 
         def widen(a, lo, hi):
             if a not in planes:
@@ -105,22 +109,12 @@ def tile_attributegnn_pb_kernel(tc, attr_rep, bwd_proj_bytes, bwd_proj_scale, se
                         out=planes[a][:, t, :], in0=src, scalar1=k_scale[:, t : t + 1], scalar2=None, op0=ALU.mult
                     )
 
-        def in_range(a):
-            return 0 <= a < A
-
         def interleave(a):
             w_group[a] = resident.tile([NP, P, PACK], BF16, name="w_group%d" % a, align_bytes=64)
-            cut = S_COLS[a]
-            if cut < P:
-                nc.vector.tensor_copy(
-                    out=w_group[a][:, cut:P, :].rearrange("p (c i) t -> p c t i", i=RUN),
-                    in_=planes[a][:, :, cut:P].rearrange("p t (c i) -> p c t i", i=RUN),
-                )
-            if cut > 0:
-                nc.scalar.copy(
-                    out=w_group[a][:, 0:cut, :].rearrange("p (c i) t -> p c t i", i=RUN),
-                    in_=planes[a][:, :, 0:cut].rearrange("p t (c i) -> p c t i", i=RUN),
-                )
+            nc.vector.tensor_copy(
+                out=w_group[a][:].rearrange("p (c i) t -> p c t i", i=RUN),
+                in_=planes[a][:].rearrange("p t (c i) -> p c t i", i=RUN),
+            )
 
         def quant_w(a):
             w_codes[a] = resident.tile([NP, P], U32, name="w_codes%d" % a, align_bytes=64)
@@ -151,57 +145,84 @@ def tile_attributegnn_pb_kernel(tc, attr_rep, bwd_proj_bytes, bwd_proj_scale, se
             nc.vector.quantize_mx(out=x_codes[a][:].bitcast(FP8X4), scales=x_scales[a][:], in_=x_group[a][:])
 
         def matmuls(a):
-            for bt in range(BT):
-                cols = slice(bt * NP, (bt + 1) * NP)
-                prod[a, bt] = psum_p.tile([NP, P], F32, name="prod", tag="prod")
-                nc.tensor.matmul_mx(
-                    out=prod[a, bt][:],
-                    lhsT=x_codes[a][:, cols].bitcast(FP8X4),
-                    lhsT_scale=x_scales[a][:, cols],
-                    rhs=w_codes[a][:].bitcast(FP8X4),
-                    rhs_scale=w_scales[a][:],
-                    start=True,
-                    stop=True,
+            for h in range(2):
+                prod[a, h] = psum_p.tile([NP, P], F32, name="prod", tag="prod")
+                if ROAD[a] == "T":
+                    for jj in range(2):
+                        cols = slice((2 * h + jj) * NP, (2 * h + jj + 1) * NP)
+                        nc.tensor.matmul_mx(
+                            out=prod[a, h][:, jj * B : (jj + 1) * B],
+                            lhsT=w_codes[a][:, cols].bitcast(FP8X4),
+                            lhsT_scale=w_scales[a][:, cols],
+                            rhs=x_codes[a][:].bitcast(FP8X4),
+                            rhs_scale=x_scales[a][:],
+                            start=True,
+                            stop=True,
+                        )
+                else:
+                    rows = slice(h * NP, (h + 1) * NP)
+                    nc.tensor.matmul_mx(
+                        out=prod[a, h][:],
+                        lhsT=x_codes[a][:, rows].bitcast(FP8X4),
+                        lhsT_scale=x_scales[a][:, rows],
+                        rhs=w_codes[a][:].bitcast(FP8X4),
+                        rhs_scale=w_scales[a][:],
+                        start=True,
+                        stop=True,
+                    )
+
+        def flags(bt):
+            first = adds_done[bt] == 0
+            adds_done[bt] += 1
+            return first, adds_done[bt] == adds_total[bt]
+
+        def empty(a, h):
+            term[a, h] = resident.tile([NP, P], F32, name="term%d_%d" % (a, h))
+            if ROAD[a] == "T":
+                nc.vector.tensor_scalar(
+                    out=term[a, h][:],
+                    in0=prod[a, h][:],
+                    scalar1=0.0,
+                    scalar2=w_f32[:, a : a + 1],
+                    op0=ALU.max,
+                    op1=ALU.mult,
                 )
-
-        def relus(a):
-            if a == 0 and PE_TYPES == 0:
-                return
-            relu[a] = resident.tile([NP, BT, P], F32, name="relu%d" % a)
-            for bt in range(BT):
-                nc.scalar.activation(out=relu[a][:, bt, :], in_=prod[a, bt][:], func=ACT.Relu)
-
-        def pe_add(a, bt):
-            nc.tensor.matmul(
-                out=pe_sum[bt][:], lhsT=diag[a][:], rhs=relu[a][:, bt, :], start=(a == 0), stop=(a == PE_TYPES - 1)
-            )
-
-        def accumulate(a):
-            w_col = w_f32[:, a : a + 1]
-            if a == 0:
-                for bt in range(BT):
-                    nc.vector.tensor_scalar(
-                        out=acc[:, bt, :], in0=prod[a, bt][:], scalar1=0.0, scalar2=w_col, op0=ALU.max, op1=ALU.mult
-                    )
-            elif a == PE_TYPES or a == A - 1:
-                for bt in range(BT):
-                    nc.vector.scalar_tensor_tensor(
-                        out=acc[:, bt, :],
-                        in0=relu[a][:, bt, :],
-                        scalar=w_col,
-                        in1=pe_sum[bt][:] if a == PE_TYPES else acc[:, bt, :],
-                        op0=ALU.mult,
-                        op1=ALU.add,
-                    )
-                    if a == A - 1:
-                        nc.sync.dma_start(out=out[bt * NP : (bt + 1) * NP, :], in_=acc[:, bt, :])
             else:
-                flat = acc[:].rearrange("p b n -> p (b n)")
-                nc.vector.scalar_tensor_tensor(
-                    out=flat, in0=relu[a][:].rearrange("p b n -> p (b n)"), scalar=w_col, in1=flat, op0=ALU.mult, op1=ALU.add
-                )
+                nc.scalar.activation(out=term[a, h][:], in_=prod[a, h][:], func=ACT.Relu)
 
-        for i in range(-max(X_AHEAD, S_AHEAD), A + 3):
+        def add(a, h):
+            if ROAD[a] == "T":
+                for jj in range(2):
+                    cols = slice((2 * h + jj) * NP, (2 * h + jj + 1) * NP)
+                    for bt in range(BT):
+                        first, last = flags(bt)
+                        nc.tensor.matmul(
+                            out=pe_sum[bt][:, cols],
+                            lhsT=term[a, h][:, jj * B + bt * NP : jj * B + (bt + 1) * NP],
+                            rhs=ident[:],
+                            is_transpose=True,
+                            start=first,
+                            stop=last,
+                        )
+            elif ROAD[a] == "D":
+                first, last = flags(h)
+                nc.tensor.matmul(out=pe_sum[h][:], lhsT=diag[a][:], rhs=term[a, h][:], start=first, stop=last)
+            else:
+                nc.vector.scalar_tensor_tensor(
+                    out=out_sb[:, h, :],
+                    in0=term[a, h][:],
+                    scalar=w_f32[:, a : a + 1],
+                    in1=pe_sum[h][:] if a == ROAD.index("V") else out_sb[:, h, :],
+                    op0=ALU.mult,
+                    op1=ALU.add,
+                )
+                if a == A - 1:
+                    nc.sync.dma_start(out=out[h * NP : (h + 1) * NP, :], in_=out_sb[:, h, :])
+
+        def road(a):
+            return ROAD[a] if in_range(a) else ""
+
+        for i in range(-max(X_AHEAD, S_AHEAD), A + 1 + V_LAG):
             if in_range(i):
                 interleave(i)
                 quant_x(i)
@@ -209,22 +230,31 @@ def tile_attributegnn_pb_kernel(tc, attr_rep, bwd_proj_bytes, bwd_proj_scale, se
                 transposes(i + X_AHEAD)
             if in_range(i + S_AHEAD):
                 widen(i + S_AHEAD, 0, min(PRE, S_PLANES[i + S_AHEAD]))
-            if in_range(i - 1):
-                relus(i - 1)
+            if road(i - 1) in ("D", "V"):
+                empty(i - 1, 0)
+                empty(i - 1, 1)
             if in_range(i + S_AHEAD):
                 widen(i + S_AHEAD, min(PRE, S_PLANES[i + S_AHEAD]), S_PLANES[i + S_AHEAD])
             if i + S_AHEAD == 0:
                 weights()
+            if i + S_AHEAD in diag:
+                make_diag(i + S_AHEAD)
             if in_range(i + V_AHEAD):
                 widen(i + V_AHEAD, S_PLANES[i + V_AHEAD], PACK)
             if in_range(i + X_AHEAD):
                 x_copy(i + X_AHEAD)
-            for a, bt in PE_ADD_AT.get(i, ()):
-                pe_add(a, bt)
-            for a in ACC_MID.get(i, ()):
-                accumulate(a)
+            if road(i - 1) == "T":
+                empty(i - 1, 0)
+                add(i - 1, 0)
             if in_range(i):
                 quant_w(i)
                 matmuls(i)
-            for a in ACC_END.get(i, ()):
-                accumulate(a)
+            if road(i - 1) == "D":
+                add(i - 1, 0)
+                add(i - 1, 1)
+            if road(i - 1) == "T":
+                empty(i - 1, 1)
+                add(i - 1, 1)
+            if road(i - V_LAG) == "V":
+                add(i - V_LAG, 0)
+                add(i - V_LAG, 1)

@@ -19,7 +19,7 @@ NP = 128
 PACK = 4
 BT = B // NP
 NT = P // NP
-RUN = 4
+RUN = 8
 
 S_PLANES = (2, 2, 3, 3, 3, 3, 3, 3)
 ROAD = "DTDTDVVV"

@@ -237,8 +237,8 @@ def tile_attributegnn_pb_kernel(tc, attr_rep, bwd_proj_bytes, bwd_proj_scale, se
                 widen(i + S_AHEAD, min(PRE, S_PLANES[i + S_AHEAD]), S_PLANES[i + S_AHEAD])
             if i + S_AHEAD == 0:
                 weights()
-            if i + S_AHEAD in diag:
-                make_diag(i + S_AHEAD)
+                for a in sorted(diag):
+                    make_diag(a)
             if in_range(i + V_AHEAD):
                 widen(i + V_AHEAD, S_PLANES[i + V_AHEAD], PACK)
             if in_range(i + X_AHEAD):

@@ -21,7 +21,7 @@ BT = B // NP
 NT = P // NP
 RUN = 8
 
-S_PLANES = (2, 2, 3, 3, 3, 3, 3, 3)
+S_PLANES = (1, 2, 3, 3, 3, 3, 3, 3)
 ROAD = "DTDTDVVV"
 V_LAG = 2
 X_AHEAD = 2
@@ -46,7 +46,8 @@ def tile_attributegnn_pb_kernel(tc, attr_rep, bwd_proj_bytes, bwd_proj_scale, se
         x_view = attr_rep.rearrange("(bt p) a k -> p bt a k", p=NP)
         w_bytes = []
         x_rows = []
-        for a in range(A):
+
+        def load_w(a):
             wb = resident.tile([NP, PACK * P], U8, name="w_bytes%d" % a)
             src = bwd_proj_bytes[a].rearrange("(p t) n -> p (t n)", t=PACK)
             if a == 0:
@@ -55,13 +56,20 @@ def tile_attributegnn_pb_kernel(tc, attr_rep, bwd_proj_bytes, bwd_proj_scale, se
             else:
                 nc.sync.dma_start(out=wb[:], in_=src)
             w_bytes.append(wb)
+
+        def load_x(a):
             xr = resident.tile([NP, BT, R], BF16, name="x_rows%d" % a)
             nc.sync.dma_start(out=xr[:], in_=x_view[:, :, a, :])
             x_rows.append(xr)
-            if a == 0:
-                nc.scalar.dma_start(
-                    out=w_bf[:], in_=self_weighted.rearrange("o a u -> (o a u)").partition_broadcast(NP)
-                )
+
+        load_w(0)
+        nc.scalar.dma_start(out=w_bf[:], in_=self_weighted.rearrange("o a u -> (o a u)").partition_broadcast(NP))
+        load_w(1)
+        load_x(0)
+        for a in range(1, A):
+            if a + 1 < A:
+                load_w(a + 1)
+            load_x(a)
 
         ident = const.tile([NP, NP], F32, name="ident")
         make_identity(nc, ident[:])
@@ -225,7 +233,6 @@ def tile_attributegnn_pb_kernel(tc, attr_rep, bwd_proj_bytes, bwd_proj_scale, se
         for i in range(-max(X_AHEAD, S_AHEAD), A + 1 + V_LAG):
             if in_range(i):
                 interleave(i)
-                quant_x(i)
             if in_range(i + X_AHEAD):
                 transposes(i + X_AHEAD)
             if in_range(i + S_AHEAD):
@@ -241,13 +248,14 @@ def tile_attributegnn_pb_kernel(tc, attr_rep, bwd_proj_bytes, bwd_proj_scale, se
                     make_diag(a)
             if in_range(i + V_AHEAD):
                 widen(i + V_AHEAD, S_PLANES[i + V_AHEAD], PACK)
-            if in_range(i + X_AHEAD):
-                x_copy(i + X_AHEAD)
+            if in_range(i + X_AHEAD - 1):
+                x_copy(i + X_AHEAD - 1)
             if road(i - 1) == "T":
                 empty(i - 1, 0)
                 add(i - 1, 0)
             if in_range(i):
                 quant_w(i)
+                quant_x(i)
                 matmuls(i)
             if road(i - 1) == "D":
                 add(i - 1, 0)

@@ -24,6 +24,7 @@ RUN = 8
 S_PLANES = (1, 2, 3, 3, 3, 3, 3, 3)
 ROAD = "DTDTDVVV"
 V_LAG = 2
+LATE_X = 2
 X_AHEAD = 2
 S_AHEAD = 2
 V_AHEAD = 1
@@ -233,6 +234,8 @@ def tile_attributegnn_pb_kernel(tc, attr_rep, bwd_proj_bytes, bwd_proj_scale, se
         for i in range(-max(X_AHEAD, S_AHEAD), A + 1 + V_LAG):
             if in_range(i):
                 interleave(i)
+                if i >= LATE_X:
+                    quant_x(i)
             if in_range(i + X_AHEAD):
                 transposes(i + X_AHEAD)
             if in_range(i + S_AHEAD):
@@ -248,14 +251,17 @@ def tile_attributegnn_pb_kernel(tc, attr_rep, bwd_proj_bytes, bwd_proj_scale, se
                     make_diag(a)
             if in_range(i + V_AHEAD):
                 widen(i + V_AHEAD, S_PLANES[i + V_AHEAD], PACK)
-            if in_range(i + X_AHEAD - 1):
+            if 0 <= i + X_AHEAD - 1 < LATE_X:
                 x_copy(i + X_AHEAD - 1)
+            if LATE_X <= i + X_AHEAD < A:
+                x_copy(i + X_AHEAD)
             if road(i - 1) == "T":
                 empty(i - 1, 0)
                 add(i - 1, 0)
             if in_range(i):
                 quant_w(i)
-                quant_x(i)
+                if i < LATE_X:
+                    quant_x(i)
                 matmuls(i)
             if road(i - 1) == "D":
                 add(i - 1, 0)

@@ -43,7 +43,10 @@ def tile_attributegnn_pb_kernel(tc, attr_rep, bwd_proj_bytes, bwd_proj_scale, se
 
         k_scale = const.tile([NP, PACK], F32, name="k_scale")
         nc.scalar.dma_start(out=k_scale[:], in_=bwd_proj_scale.rearrange("o (p t) u -> p (o t u)", t=PACK))
-        w_bf = const.tile([NP, A], BF16, name="w_bf")
+        w_row = const.tile([NP, A], BF16, name="w_row")
+        ones = const.tile([NP, NP], BF16, name="ones")
+        nc.vector.memset(w_row[:], 0.0)
+        nc.vector.memset(ones[:], 1.0)
         x_view = attr_rep.rearrange("(bt p) a k -> p bt a k", p=NP)
         w_bytes = []
         x_rows = []
@@ -64,7 +67,7 @@ def tile_attributegnn_pb_kernel(tc, attr_rep, bwd_proj_bytes, bwd_proj_scale, se
             x_rows.append(xr)
 
         load_w(0)
-        nc.scalar.dma_start(out=w_bf[:], in_=self_weighted.rearrange("o a u -> (o a u)").partition_broadcast(NP))
+        nc.scalar.dma_start(out=w_row[0:1, :], in_=self_weighted.rearrange("o a u -> o (a u)"))
         load_w(1)
         load_x(0)
         for a in range(1, A):
@@ -81,8 +84,11 @@ def tile_attributegnn_pb_kernel(tc, attr_rep, bwd_proj_bytes, bwd_proj_scale, se
         w_f32 = const.tile([NP, A], F32, name="w_f32")
         diag = dict((a, const.tile([NP, NP], F32, name="diag%d" % a)) for a in range(A) if ROAD[a] == "D")
 
+        w_ps = psum_p.tile([NP, P], F32, name="prod", tag="prod")
+        nc.tensor.matmul(out=w_ps[:, 0:A], lhsT=ones[:], rhs=w_row[:], start=True, stop=True)
+
         def weights():
-            nc.scalar.activation(out=w_f32[:], in_=w_bf[:], func=ACT.Copy)
+            nc.scalar.activation(out=w_f32[:], in_=w_ps[:, 0:A], func=ACT.Copy)
 
         def make_diag(a):
             nc.scalar.activation(out=diag[a][:], in_=ident[:], func=ACT.Copy, scale=w_f32[:, a : a + 1])

from contextlib import ExitStack

import concourse.mybir as mybir
from concourse.masks import make_identity

B, A, R, P = 256, 8, 512, 512
FLOPS = 2 * B * A * R * P

F32 = mybir.dt.float32
BF16 = mybir.dt.bfloat16
U32 = mybir.dt.uint32
U8 = mybir.dt.uint8
FP8 = mybir.dt.float8_e4m3fn
FP8X4 = mybir.dt.float8_e4m3fn_x4
ALU = mybir.AluOpType
ACT = mybir.ActivationFunctionType

NP = 128
PACK = 4
BT = B // NP
NT = P // NP
RUN = 8

S_PLANES = (1, 2, 3, 3, 3, 3, 3, 3)
ROAD = "DTDTDVVV"
V_LAG = 2
LATE_X = 2
X_AHEAD = 2
S_AHEAD = 2
V_AHEAD = 1
PRE = 1


def tile_attributegnn_pb_kernel(tc, attr_rep, bwd_proj_bytes, bwd_proj_scale, self_weighted, out):
    nc = tc.nc
    with ExitStack() as ctx:
        const = ctx.enter_context(tc.tile_pool(name="const", bufs=1))
        resident = ctx.enter_context(tc.tile_pool(name="resident", bufs=1))
        psum_x = ctx.enter_context(tc.psum_pool(name="psum_x", bufs=2))
        psum_p = ctx.enter_context(tc.psum_pool(name="psum_p", bufs=4))
        psum_s = ctx.enter_context(tc.psum_pool(name="psum_s", bufs=1))
        ctx.enter_context(tc.manual_schedule())

        k_scale = const.tile([NP, PACK], F32, name="k_scale")
        nc.scalar.dma_start(out=k_scale[:], in_=bwd_proj_scale.rearrange("o (p t) u -> p (o t u)", t=PACK))
        w_row = const.tile([NP, A], BF16, name="w_row")
        ones = const.tile([NP, NP], BF16, name="ones")
        nc.vector.memset(w_row[:], 0.0)
        nc.vector.memset(ones[:], 1.0)
        x_view = attr_rep.rearrange("(bt p) a k -> p bt a k", p=NP)
        w_bytes = []
        x_rows = []

        def load_w(a):
            wb = resident.tile([NP, PACK * P], U8, name="w_bytes%d" % a)
            src = bwd_proj_bytes[a].rearrange("(p t) n -> p (t n)", t=PACK)
            if a == 0:
                for t in range(PACK):
                    nc.sync.dma_start(out=wb[:, t * P : (t + 1) * P], in_=src[:, t * P : (t + 1) * P])
            else:
                nc.sync.dma_start(out=wb[:], in_=src)
            w_bytes.append(wb)

        def load_x(a):
            xr = resident.tile([NP, BT, R], BF16, name="x_rows%d" % a)
            nc.sync.dma_start(out=xr[:], in_=x_view[:, :, a, :])
            x_rows.append(xr)

        load_w(0)
        nc.scalar.dma_start(out=w_row[0:1, :], in_=self_weighted.rearrange("o a u -> o (a u)"))
        load_w(1)
        load_x(0)
        for a in range(1, A):
            if a + 1 < A:
                load_w(a + 1)
            load_x(a)

        ident = const.tile([NP, NP], F32, name="ident")
        make_identity(nc, ident[:])
        warm_in = const.tile([NP, 1], F32, name="warm_in")
        warm_out = const.tile([NP, 1], F32, name="warm_out")
        nc.vector.memset(warm_in[:], 0.0)
        nc.scalar.activation(out=warm_out[:], in_=warm_in[:], func=ACT.Relu)
        w_f32 = const.tile([NP, A], F32, name="w_f32")
        diag = dict((a, const.tile([NP, NP], F32, name="diag%d" % a)) for a in range(A) if ROAD[a] == "D")

        w_ps = psum_p.tile([NP, P], F32, name="prod", tag="prod")
        nc.tensor.matmul(out=w_ps[:, 0:A], lhsT=ones[:], rhs=w_row[:], start=True, stop=True)

        def weights():
            nc.scalar.activation(out=w_f32[:], in_=w_ps[:, 0:A], func=ACT.Copy)

        def make_diag(a):
            nc.scalar.activation(out=diag[a][:], in_=ident[:], func=ACT.Copy, scale=w_f32[:, a : a + 1])

        out_sb = const.tile([NP, BT, P], F32, name="out_sb")
        pe_sum = [psum_s.tile([NP, P], F32, name="pe_sum%d" % bt) for bt in range(BT)]
        adds_total = [NT * ROAD.count("T") + ROAD.count("D")] * BT
        adds_done = [0, 0]

        planes = {}
        w_group = {}
        w_codes = {}
        w_scales = {}
        x_t = {}
        x_group = {}
        x_codes = {}
        x_scales = {}
        prod = {}
        term = {}

        def in_range(a):
            return 0 <= a < A

        def widen(a, lo, hi):
            if a not in planes:
                planes[a] = resident.tile([NP, PACK, P], BF16, name="planes%d" % a)
            for t in range(lo, hi):
                src = w_bytes[a][:, t * P : (t + 1) * P].bitcast(FP8)
                if t < S_PLANES[a]:
                    nc.scalar.activation(out=planes[a][:, t, :], in_=src, func=ACT.Copy, scale=k_scale[:, t : t + 1])
                else:
                    nc.vector.tensor_scalar(
                        out=planes[a][:, t, :], in0=src, scalar1=k_scale[:, t : t + 1], scalar2=None, op0=ALU.mult
                    )

        def interleave(a):
            w_group[a] = resident.tile([NP, P, PACK], BF16, name="w_group%d" % a, align_bytes=64)
            nc.vector.tensor_copy(
                out=w_group[a][:].rearrange("p (c i) t -> p c t i", i=RUN),
                in_=planes[a][:].rearrange("p t (c i) -> p c t i", i=RUN),
            )

        def quant_w(a):
            w_codes[a] = resident.tile([NP, P], U32, name="w_codes%d" % a, align_bytes=64)
            w_scales[a] = resident.tile([NP, P], U8, name="w_scales%d" % a, align_bytes=64)
            nc.vector.quantize_mx(
                out=w_codes[a][:].bitcast(FP8X4),
                scales=w_scales[a][:],
                in_=w_group[a][:].rearrange("p n t -> p (n t)"),
            )

        def transposes(a):
            x_t[a] = psum_x.tile([NP, 2, B], F32, name="x_t", tag="x_t")
            for bt in range(BT):
                words = x_rows[a][:, bt, :].bitcast(F32)
                for u in range(2):
                    nc.tensor.transpose(x_t[a][:, u, bt * NP : (bt + 1) * NP], words[:, u : R // 2 : 2], ident[:])

        def x_copy(a):
            x_group[a] = resident.tile([NP, B * PACK], BF16, name="x_group%d" % a, align_bytes=64)
            nc.scalar.copy(
                out=x_group[a][:].bitcast(F32).rearrange("p (b u) -> p b u", u=2),
                in_=x_t[a][:].rearrange("p u b -> p b u"),
            )

        def quant_x(a):
            x_codes[a] = resident.tile([NP, B], U32, name="x_codes%d" % a, align_bytes=64)
            x_scales[a] = resident.tile([NP, B], U8, name="x_scales%d" % a, align_bytes=64)
            nc.vector.quantize_mx(out=x_codes[a][:].bitcast(FP8X4), scales=x_scales[a][:], in_=x_group[a][:])

        def matmuls(a):
            for h in range(2):
                prod[a, h] = psum_p.tile([NP, P], F32, name="prod", tag="prod")
                if ROAD[a] == "T":
                    for jj in range(2):
                        cols = slice((2 * h + jj) * NP, (2 * h + jj + 1) * NP)
                        nc.tensor.matmul_mx(
                            out=prod[a, h][:, jj * B : (jj + 1) * B],
                            lhsT=w_codes[a][:, cols].bitcast(FP8X4),
                            lhsT_scale=w_scales[a][:, cols],
                            rhs=x_codes[a][:].bitcast(FP8X4),
                            rhs_scale=x_scales[a][:],
                            start=True,
                            stop=True,
                        )
                else:
                    rows = slice(h * NP, (h + 1) * NP)
                    nc.tensor.matmul_mx(
                        out=prod[a, h][:],
                        lhsT=x_codes[a][:, rows].bitcast(FP8X4),
                        lhsT_scale=x_scales[a][:, rows],
                        rhs=w_codes[a][:].bitcast(FP8X4),
                        rhs_scale=w_scales[a][:],
                        start=True,
                        stop=True,
                    )

        def flags(bt):
            first = adds_done[bt] == 0
            adds_done[bt] += 1
            return first, adds_done[bt] == adds_total[bt]

        def empty(a, h):
            term[a, h] = resident.tile([NP, P], F32, name="term%d_%d" % (a, h))
            if ROAD[a] == "T":
                nc.vector.tensor_scalar(
                    out=term[a, h][:],
                    in0=prod[a, h][:],
                    scalar1=0.0,
                    scalar2=w_f32[:, a : a + 1],
                    op0=ALU.max,
                    op1=ALU.mult,
                )
            else:
                nc.scalar.activation(out=term[a, h][:], in_=prod[a, h][:], func=ACT.Relu)

        def add(a, h):
            if ROAD[a] == "T":
                for jj in range(2):
                    cols = slice((2 * h + jj) * NP, (2 * h + jj + 1) * NP)
                    for bt in range(BT):
                        first, last = flags(bt)
                        nc.tensor.matmul(
                            out=pe_sum[bt][:, cols],
                            lhsT=term[a, h][:, jj * B + bt * NP : jj * B + (bt + 1) * NP],
                            rhs=ident[:],
                            is_transpose=True,
                            start=first,
                            stop=last,
                        )
            elif ROAD[a] == "D":
                first, last = flags(h)
                nc.tensor.matmul(out=pe_sum[h][:], lhsT=diag[a][:], rhs=term[a, h][:], start=first, stop=last)
            else:
                nc.vector.scalar_tensor_tensor(
                    out=out_sb[:, h, :],
                    in0=term[a, h][:],
                    scalar=w_f32[:, a : a + 1],
                    in1=pe_sum[h][:] if a == ROAD.index("V") else out_sb[:, h, :],
                    op0=ALU.mult,
                    op1=ALU.add,
                )
                if a == A - 1:
                    nc.sync.dma_start(out=out[h * NP : (h + 1) * NP, :], in_=out_sb[:, h, :])

        def road(a):
            return ROAD[a] if in_range(a) else ""

        for i in range(-max(X_AHEAD, S_AHEAD), A + 1 + V_LAG):
            if in_range(i):
                interleave(i)
                if i >= LATE_X:
                    quant_x(i)
            if in_range(i + X_AHEAD):
                transposes(i + X_AHEAD)
            if in_range(i + S_AHEAD):
                widen(i + S_AHEAD, 0, min(PRE, S_PLANES[i + S_AHEAD]))
            if road(i - 1) in ("D", "V"):
                empty(i - 1, 0)
                empty(i - 1, 1)
            if in_range(i + S_AHEAD):
                widen(i + S_AHEAD, min(PRE, S_PLANES[i + S_AHEAD]), S_PLANES[i + S_AHEAD])
            if i + S_AHEAD == 0:
                weights()
                for a in sorted(diag):
                    make_diag(a)
            if in_range(i + V_AHEAD):
                widen(i + V_AHEAD, S_PLANES[i + V_AHEAD], PACK)
            if 0 <= i + X_AHEAD - 1 < LATE_X:
                x_copy(i + X_AHEAD - 1)
            if LATE_X <= i + X_AHEAD < A:
                x_copy(i + X_AHEAD)
            if road(i - 1) == "T":
                empty(i - 1, 0)
                add(i - 1, 0)
            if in_range(i):
                quant_w(i)
                if i < LATE_X:
                    quant_x(i)
                matmuls(i)
            if road(i - 1) == "D":
                add(i - 1, 0)
                add(i - 1, 1)
            if road(i - 1) == "T":
                empty(i - 1, 1)
                add(i - 1, 1)
            if road(i - V_LAG) == "V":
                add(i - V_LAG, 0)
                add(i - V_LAG, 1)
